import numpy as np
import ml_dtypes


def mxq(x, axis, fmt="e4m3"):
    dtype, down = {"e4m3": (ml_dtypes.float8_e4m3fn, 7), "e5m2": (ml_dtypes.float8_e5m2, 14)}[fmt]
    v = np.moveaxis(np.asarray(x, np.float32).astype(ml_dtypes.bfloat16).astype(np.float64), axis, -1)
    blocks = v.reshape(v.shape[:-1] + (-1, 32))
    amax = np.abs(blocks).max(-1, keepdims=True)
    byte = np.maximum(np.where(amax > 0, np.frexp(amax)[1] - 1 + 127, 0) - down, 1)
    scale = np.exp2(byte - 127.0)
    codes = (blocks / scale).astype(np.float32).astype(dtype).astype(np.float64)
    return np.moveaxis((codes * scale).reshape(v.shape), -1, axis)


WIDE = False


def mx_kscale(k):
    if not WIDE:
        return np.ones(k)
    levels = np.array([10, -10, 5, -5, 0])
    a = np.random.permutation(np.resize(levels, k // 512 * 4)).reshape(k // 512, 4)
    idx = np.arange(k)
    return np.exp2(a[idx // 512, idx % 128 // 32])


BF16 = ml_dtypes.bfloat16


def bf(x):
    return np.asarray(x, np.float32).astype(BF16)


def f64(x):
    return np.asarray(x).astype(np.float64)


E2M1 = np.array([0.0, 0.5, 1.0, 1.5, 2.0, 3.0, 4.0, 6.0, -0.0, -0.5, -1.0, -1.5, -2.0, -3.0, -4.0, -6.0])


def pack_weight(w, fmt):
    k, n = w.shape
    w = f64(bf(w)).reshape(k // 32, 32, n)
    amax = np.abs(w).max(1)
    if fmt == "e4m3":
        byte = np.frexp(amax)[1] - 1 + 127 - 7
    else:
        mant, ex = np.frexp(amax / 6.0)
        byte = np.where(mant > 0.5, ex, ex - 1) + 127
    byte = np.clip(np.where(amax > 0, byte, 1), 1, 254)
    scaled = (w * np.exp2(127.0 - byte)[:, None, :]).reshape(k, n).astype(np.float32)
    by_word = np.ascontiguousarray(scaled.reshape(k // 512, 128, 4, n).transpose(0, 1, 3, 2))
    if fmt == "e4m3":
        words = by_word.astype(ml_dtypes.float8_e4m3fn).view(np.uint8)
    else:
        c = by_word.astype(ml_dtypes.float4_e2m1fn).view(np.uint8) & 0xF
        words = c[..., 0::2] | (c[..., 1::2] << 4)
    return np.ascontiguousarray(words), np.ascontiguousarray(byte.astype(np.uint8).reshape(k // 512, 16, n))


def unpack_weight(words, scales, fmt):
    g, p, n, _ = words.shape
    if fmt == "e4m3":
        vals = np.ascontiguousarray(words).view(ml_dtypes.float8_e4m3fn).astype(np.float64)
    else:
        nib = np.empty((g, p, n, 4), np.uint8)
        nib[..., 0::2] = words & 0xF
        nib[..., 1::2] = words >> 4
        vals = E2M1[nib]
    vals = vals * np.repeat(np.exp2(scales.astype(np.float64) - 127.0), 8, axis=1)[..., None]
    return vals.transpose(0, 1, 3, 2).reshape(g * 512, n)


M, N, E, P, S, B, KT = 512, 512, 4, 32, 17, 4096, 2


def setup_inputs():
    s = mx_kscale(M)
    z = bf(np.random.standard_normal((M, B)) * s[:, None])
    mlp_out = bf(np.random.standard_normal((B, E)) * 0.65)
    t2 = bf(0.5 + 0.1 * np.random.random_sample(1))
    A = bf(np.random.standard_normal((E, M)) * 0.5 / s)
    W = np.random.standard_normal((E, M, M)) / np.sqrt(M) / s
    h = bf(np.random.standard_normal((E, M)) * 0.1)
    cat = np.ascontiguousarray(W.swapaxes(1, 2)).reshape(-1, M)
    W_words, W_scales = pack_weight(cat, "e4m3")
    return {
        "z": z,
        "mlp_out": mlp_out,
        "t2": t2,
        "A": A,
        "W_words": W_words,
        "W_scales": W_scales,
        "h": h,
    }


def reference(z, mlp_out, t2, A, W_words, W_scales, h):
    z = f64(z)
    lg = -f64(mlp_out).T / f64(t2)[0]
    ex = np.exp(lg - lg.max(axis=0, keepdims=True))
    w_exp = ex / ex.sum(axis=0, keepdims=True)
    zcat = np.concatenate([z[:-P], np.maximum(z[-P:], 0.0)], axis=0)
    Az = f64(A)[:, :, None] * z[None, :, :]
    Wz = unpack_weight(W_words, W_scales, "e4m3").reshape(E, M, M).swapaxes(1, 2) @ mxq(zcat, 0, "e4m3")
    expert_out = Az + Wz + f64(h)[:, :, None]
    return np.sum(expert_out * w_exp[:, None, :], axis=0)

@@ -1,0 +1,275 @@
+from contextlib import ExitStack
+
+import concourse.mybir as mybir
+from concourse.masks import make_identity
+
+F32 = mybir.dt.float32
+BF16 = mybir.dt.bfloat16
+I32 = mybir.dt.int32
+U32 = mybir.dt.uint32
+U8 = mybir.dt.uint8
+FP8X4 = mybir.dt.float8_e4m3fn_x4
+ALU = mybir.AluOpType
+ACT = mybir.ActivationFunctionType
+AX = mybir.AxisListType
+
+P = 128
+PACK = 4
+E = 4
+M = 512
+B = 4096
+RELU_ROWS = 32
+N_TILES = B // P
+CHUNK = 512
+TILES_PER_CHUNK = CHUNK // P
+LOAD_COLS = 1024
+PIECES = 3
+PLAIN_H_GROUPS = 2
+TILES_PER_BANK = 8
+BF16_MAX = 3.3895313892515355e38
+
+FLOPS = 2 * E * M * M * B
+
+
+def tile_dynamix_pb_t_e_kernel(tc, z, mlp_out, t2, A, W_words, W_scales, h, out):
+    nc = tc.nc
+    with ExitStack() as ctx:
+        ctx.enter_context(tc.manual_schedule())
+        keep = ctx.enter_context(tc.tile_pool(name="keep", bufs=1))
+        work = ctx.enter_context(tc.tile_pool(name="work", bufs=3))
+        psum_p = ctx.enter_context(tc.psum_pool(name="psum_p", bufs=1))
+        psum_g = ctx.enter_context(tc.psum_pool(name="psum_g", bufs=2))
+        psum_f = ctx.enter_context(tc.psum_pool(name="psum_f", bufs=2))
+
+        z_rows = z.rearrange("(q t) b -> q t b", t=PACK)
+        out_rows = out.rearrange("(q t) b -> q t b", t=PACK)
+
+        mlp_sb = keep.tile([P, N_TILES, E], BF16)
+        t2_sb = keep.tile([P, 1], BF16)
+        a_rows = keep.tile([P, M], BF16)
+        h_rows = keep.tile([P, M], BF16)
+        h_all = keep.tile([P, E, M], BF16)
+        z_raw = keep.tile([P, PACK, B], BF16)
+        w_words = keep.tile([P, E, M], U32, align_bytes=64)
+        w_planes = keep.tile([P, E, M], U8, align_bytes=64)
+        gate_pad = keep.tile([P, N_TILES, P], BF16)
+        warm = keep.tile([P, 1], F32)
+
+        nc.vector.memset(w_planes[:].rearrange("p g n -> p (g n)").bitcast(I32), 0)
+        nc.vector.memset(a_rows[:], 0.0)
+        nc.vector.memset(h_rows[:], 0.0)
+        nc.vector.memset(warm[:], 0.0)
+        nc.vector.memset(gate_pad[:].rearrange("p c j -> p (c j)").bitcast(I32), 0)
+
+        nc.scalar.dma_start(out=mlp_sb[:], in_=mlp_out.rearrange("(c p) e -> p c e", p=P))
+        nc.scalar.dma_start(out=t2_sb[:], in_=t2.partition_broadcast(P))
+        for i in range(PIECES):
+            nc.scalar.dma_start(out=a_rows[E * i : E * (i + 1), :], in_=A)
+            nc.scalar.dma_start(out=h_rows[E * i : E * (i + 1), :], in_=h)
+        nc.scalar.dma_start(out=h_all[:], in_=h.partition_broadcast(P))
+        nc.scalar.activation(out=warm[:], in_=warm[:], func=ACT.Exp)
+
+        for quad in range(4):
+            nc.sync.dma_start(
+                out=w_planes[32 * quad : 32 * quad + 4, :, :].bitcast(I32),
+                in_=W_scales.bitcast(I32)[:, 4 * quad : 4 * quad + 4, :].rearrange("g r n -> r g n"),
+            )
+        nc.sync.dma_start(out=z_raw[:, :, 0:LOAD_COLS], in_=z_rows[:, :, 0:LOAD_COLS])
+        for g in range(E):
+            nc.sync.dma_start(
+                out=w_words[:, g, :].bitcast(I32),
+                in_=W_words[g].rearrange("p n t -> p (n t)").bitcast(I32),
+            )
+        for first in range(LOAD_COLS, B, LOAD_COLS):
+            nc.sync.dma_start(
+                out=z_raw[:, :, first : first + LOAD_COLS], in_=z_rows[:, :, first : first + LOAD_COLS]
+            )
+
+        ident_f = keep.tile([P, P], F32)
+        make_identity(nc, ident_f[:])
+        ident_b = keep.tile([P, P], BF16)
+        make_identity(nc, ident_b[:])
+        relu_flag = keep.tile([P, 1], F32)
+        nc.vector.tensor_reduce(
+            out=relu_flag[:], in_=ident_f[:, P - RELU_ROWS // PACK : P], axis=AX.X, op=ALU.add
+        )
+        floor = keep.tile([P, 1], F32)
+        nc.vector.tensor_scalar(
+            out=floor[:], in0=relu_flag[:], scalar1=BF16_MAX, scalar2=-BF16_MAX, op0=ALU.mult, op1=ALU.add
+        )
+
+        t2_f = keep.tile([P, 1], F32)
+        nc.vector.tensor_copy(out=t2_f[:], in_=t2_sb[:])
+        inv_t2 = keep.tile([P, 1], F32)
+        nc.vector.reciprocal(out=inv_t2[:], in_=t2_f[:])
+        logit = keep.tile([P, N_TILES, E], F32)
+        nc.vector.tensor_scalar(
+            out=logit[:], in0=mlp_sb[:], scalar1=inv_t2[:, 0:1], scalar2=-1.0, op0=ALU.mult, op1=ALU.mult
+        )
+        top = keep.tile([P, N_TILES], F32)
+        nc.vector.tensor_reduce(out=top[:], in_=logit[:], axis=AX.X, op=ALU.max)
+        nc.vector.tensor_tensor(
+            out=logit[:], in0=logit[:], in1=top[:].unsqueeze(2).to_broadcast([P, N_TILES, E]), op=ALU.subtract
+        )
+        expd = keep.tile([P, N_TILES, E], F32)
+        nc.scalar.activation(out=expd[:], in_=logit[:], func=ACT.Exp)
+        total = keep.tile([P, N_TILES], F32)
+        nc.vector.tensor_reduce(out=total[:], in_=expd[:], axis=AX.X, op=ALU.add)
+        inv_total = keep.tile([P, N_TILES], F32)
+        nc.vector.reciprocal(out=inv_total[:], in_=total[:])
+        gate = keep.tile([P, N_TILES, E], F32)
+        nc.vector.tensor_tensor(
+            out=gate[:], in0=expd[:], in1=inv_total[:].unsqueeze(2).to_broadcast([P, N_TILES, E]), op=ALU.mult
+        )
+
+        rest = gate
+        for i in range(PIECES):
+            piece = gate_pad[:, :, E * i : E * (i + 1)]
+            nc.vector.tensor_copy(out=piece, in_=rest[:])
+            if i + 1 < PIECES:
+                smaller = keep.tile([P, N_TILES, E], F32, name="rest%d" % i)
+                nc.vector.tensor_tensor(out=smaller[:], in0=rest[:], in1=piece, op=ALU.subtract)
+                rest = smaller
+        a_stat = keep.tile([P, PACK, P], BF16)
+        h_stat = keep.tile([P, PACK, P], BF16)
+        nc.vector.tensor_copy(out=a_stat[:], in_=a_rows[:].rearrange("j (q t) -> j t q", t=PACK))
+        nc.vector.tensor_copy(out=h_stat[:], in_=h_rows[:].rearrange("j (q t) -> j t q", t=PACK))
+        gate_rows = keep.tile([P, B], BF16)
+        for first in range(0, N_TILES, TILES_PER_BANK):
+            rows_ps = psum_g.tile([P, TILES_PER_BANK * P], BF16, tag="g_ps")
+            for j in range(TILES_PER_BANK):
+                nc.tensor.transpose(rows_ps[:, P * j : P * (j + 1)], gate_pad[:, first + j, :], ident_b[:])
+            nc.scalar.copy(out=gate_rows[:, P * first : P * (first + TILES_PER_BANK)], in_=rows_ps[:])
+
+        z_codes = keep.tile([P, B], U32, align_bytes=64)
+        z_scales = keep.tile([P, B], U8, align_bytes=64)
+        out_sb = keep.tile([P, PACK, B], F32)
+        grouped = {}
+        leaves = {}
+        mixed = {}
+        h_tiles = {}
+        back = {}
+
+        def tile_cols(c):
+            return slice(c * P, (c + 1) * P)
+
+        def regroup(c):
+            grouped[c] = work.tile([P, P, PACK], BF16, align_bytes=64, name="grouped")
+            nc.vector.tensor_scalar(
+                out=grouped[c][:],
+                in0=z_raw[:, :, tile_cols(c)].rearrange("q t b -> q b t"),
+                scalar1=floor[:, 0:1],
+                scalar2=None,
+                op0=ALU.max,
+            )
+
+        def quantise(c):
+            nc.vector.quantize_mx(
+                out=z_codes[:, tile_cols(c)].bitcast(FP8X4),
+                scales=z_scales[:, tile_cols(c)],
+                in_=grouped[c][:].rearrange("q b t -> q (b t)"),
+            )
+
+        def a_term(i):
+            t = i % PACK
+            cols = slice((i // PACK) * CHUNK, (i // PACK + 1) * CHUNK)
+            g_ps = psum_g.tile([P, CHUNK], F32, tag="g_ps")
+            nc.tensor.matmul(out=g_ps[:], lhsT=a_stat[:, t, :], rhs=gate_rows[:, cols], start=True, stop=True)
+            nc.vector.tensor_tensor(out=out_sb[:, t, cols], in0=g_ps[:], in1=z_raw[:, t, cols], op=ALU.mult)
+
+        def experts(c):
+            leaves[c] = []
+            for e in range(E):
+                p_ps = psum_p.tile([P, M], F32, name="p_ps%d" % e)
+                nc.tensor.matmul_mx(
+                    out=p_ps[:],
+                    lhsT=z_codes[:, tile_cols(c)].bitcast(FP8X4),
+                    lhsT_scale=z_scales[:, tile_cols(c)],
+                    rhs=w_words[:, e, :].bitcast(FP8X4),
+                    rhs_scale=w_planes[:, e, :],
+                    start=True,
+                    stop=True,
+                )
+                leaves[c].append(p_ps[:].rearrange("b (q t) -> b t q", t=PACK))
+
+        def mix(c):
+            s0 = work.tile([P, PACK, P], F32)
+            s2 = work.tile([P, PACK, P], F32)
+            s01 = work.tile([P, PACK, P], F32)
+            s23 = work.tile([P, PACK, P], F32)
+            mixed[c] = work.tile([P, PACK, P], F32, name="mixed")
+            nc.scalar.activation(out=s0[:], in_=leaves[c][0], func=ACT.Copy, scale=gate[:, c, 0:1])
+            nc.scalar.activation(out=s2[:], in_=leaves[c][2], func=ACT.Copy, scale=gate[:, c, 2:3])
+            nc.vector.scalar_tensor_tensor(
+                out=s01[:], in0=leaves[c][1], scalar=gate[:, c, 1:2], in1=s0[:], op0=ALU.mult, op1=ALU.add
+            )
+            nc.vector.scalar_tensor_tensor(
+                out=s23[:], in0=leaves[c][3], scalar=gate[:, c, 3:4], in1=s2[:], op0=ALU.mult, op1=ALU.add
+            )
+            nc.gpsimd.tensor_tensor(out=mixed[c][:], in0=s01[:], in1=s23[:], op=ALU.add)
+
+        def gated_h(c):
+            h_tiles[c] = []
+            for e in range(E):
+                gh = work.tile([P, PACK - PLAIN_H_GROUPS, P], F32, name="gh%d" % e)
+                nc.scalar.activation(
+                    out=gh[:],
+                    in_=h_all[:, e, :].rearrange("b (q t) -> b t q", t=PACK)[:, PLAIN_H_GROUPS:PACK, :],
+                    func=ACT.Copy,
+                    scale=gate[:, c, e : e + 1],
+                )
+                h_tiles[c].append(gh)
+
+        def turn_back(c):
+            back[c] = psum_f.tile([P, PACK, P], F32, name="f_ps")
+            for t in range(PACK):
+                nc.tensor.matmul(
+                    out=back[c][:, t, :], lhsT=mixed[c][:, t, :], rhs=ident_f[:], start=True, stop=False, is_transpose=True
+                )
+                if t < PLAIN_H_GROUPS:
+                    nc.tensor.matmul(
+                        out=back[c][:, t, :], lhsT=h_stat[:, t, :], rhs=gate_rows[:, tile_cols(c)], start=False, stop=True
+                    )
+                else:
+                    for e in range(E):
+                        nc.tensor.matmul(
+                            out=back[c][:, t, :],
+                            lhsT=h_tiles[c][e][:, t - PLAIN_H_GROUPS, :],
+                            rhs=ident_f[:],
+                            start=False,
+                            stop=(e == E - 1),
+                            is_transpose=True,
+                        )
+
+        def finish(c):
+            nc.vector.tensor_tensor(
+                out=out_sb[:, :, tile_cols(c)], in0=back[c][:], in1=out_sb[:, :, tile_cols(c)], op=ALU.add
+            )
+            if c % TILES_PER_CHUNK == TILES_PER_CHUNK - 1:
+                cols = slice((c + 1) * P - CHUNK, (c + 1) * P)
+                nc.sync.dma_start(out=out_rows[:, :, cols], in_=out_sb[:, :, cols])
+
+        regroup(0)
+        regroup(1)
+        quantise(0)
+        regroup(2)
+        quantise(1)
+        gated_h(0)
+        for i in range(PACK):
+            a_term(i)
+        for c in range(N_TILES + 1):
+            if c < N_TILES:
+                experts(c)
+                mix(c)
+            if c + 1 < N_TILES:
+                gated_h(c + 1)
+            if c >= 1:
+                turn_back(c - 1)
+            if c + PACK < N_TILES:
+                a_term(c + PACK)
+            if c >= 1:
+                finish(c - 1)
+            if c + 3 < N_TILES:
+                regroup(c + 3)
+            if c + 2 < N_TILES:
+                quantise(c + 2)

@@ -21,10 +21,11 @@ B = 4096
 RELU_ROWS = 32
 N_TILES = B // P
 CHUNK = 512
+N_CHUNKS = B // CHUNK
 TILES_PER_CHUNK = CHUNK // P
-LOAD_COLS = 1024
 PIECES = 3
 PLAIN_H_GROUPS = 2
+RUN = 4
 TILES_PER_BANK = 8
 BF16_MAX = 3.3895313892515355e38
 
@@ -37,6 +38,8 @@ def tile_dynamix_pb_t_e_kernel(tc, z, mlp_out, t2, A, W_words, W_scales, h, out)
         ctx.enter_context(tc.manual_schedule())
         keep = ctx.enter_context(tc.tile_pool(name="keep", bufs=1))
         work = ctx.enter_context(tc.tile_pool(name="work", bufs=3))
+        z_pool = ctx.enter_context(tc.tile_pool(name="z_pool", bufs=N_CHUNKS))
+        out_pool = ctx.enter_context(tc.tile_pool(name="out_pool", bufs=3))
         psum_p = ctx.enter_context(tc.psum_pool(name="psum_p", bufs=1))
         psum_g = ctx.enter_context(tc.psum_pool(name="psum_g", bufs=2))
         psum_f = ctx.enter_context(tc.psum_pool(name="psum_f", bufs=2))
@@ -49,7 +52,6 @@ def tile_dynamix_pb_t_e_kernel(tc, z, mlp_out, t2, A, W_words, W_scales, h, out)
         a_rows = keep.tile([P, M], BF16)
         h_rows = keep.tile([P, M], BF16)
         h_all = keep.tile([P, E, M], BF16)
-        z_raw = keep.tile([P, PACK, B], BF16)
         w_words = keep.tile([P, E, M], U32, align_bytes=64)
         w_planes = keep.tile([P, E, M], U8, align_bytes=64)
         gate_pad = keep.tile([P, N_TILES, P], BF16)
@@ -63,10 +65,6 @@ def tile_dynamix_pb_t_e_kernel(tc, z, mlp_out, t2, A, W_words, W_scales, h, out)
 
         nc.scalar.dma_start(out=mlp_sb[:], in_=mlp_out.rearrange("(c p) e -> p c e", p=P))
         nc.scalar.dma_start(out=t2_sb[:], in_=t2.partition_broadcast(P))
-        for i in range(PIECES):
-            nc.scalar.dma_start(out=a_rows[E * i : E * (i + 1), :], in_=A)
-            nc.scalar.dma_start(out=h_rows[E * i : E * (i + 1), :], in_=h)
-        nc.scalar.dma_start(out=h_all[:], in_=h.partition_broadcast(P))
         nc.scalar.activation(out=warm[:], in_=warm[:], func=ACT.Exp)
 
         for quad in range(4):
@@ -74,16 +72,25 @@ def tile_dynamix_pb_t_e_kernel(tc, z, mlp_out, t2, A, W_words, W_scales, h, out)
                 out=w_planes[32 * quad : 32 * quad + 4, :, :].bitcast(I32),
                 in_=W_scales.bitcast(I32)[:, 4 * quad : 4 * quad + 4, :].rearrange("g r n -> r g n"),
             )
-        nc.sync.dma_start(out=z_raw[:, :, 0:LOAD_COLS], in_=z_rows[:, :, 0:LOAD_COLS])
+        z_raw = []
+
+        def load_z(k):
+            z_chunk = z_pool.tile([P, PACK, CHUNK], BF16)
+            nc.sync.dma_start(out=z_chunk[:], in_=z_rows[:, :, k * CHUNK : (k + 1) * CHUNK])
+            z_raw.append(z_chunk)
+
+        load_z(0)
         for g in range(E):
             nc.sync.dma_start(
                 out=w_words[:, g, :].bitcast(I32),
                 in_=W_words[g].rearrange("p n t -> p (n t)").bitcast(I32),
             )
-        for first in range(LOAD_COLS, B, LOAD_COLS):
-            nc.sync.dma_start(
-                out=z_raw[:, :, first : first + LOAD_COLS], in_=z_rows[:, :, first : first + LOAD_COLS]
-            )
+        nc.sync.dma_start(out=h_all[:], in_=h.partition_broadcast(P))
+        for i in range(PIECES):
+            nc.sync.dma_start(out=a_rows[E * i : E * (i + 1), :], in_=A)
+            nc.sync.dma_start(out=h_rows[E * i : E * (i + 1), :], in_=h)
+        for k in range(1, N_CHUNKS):
+            load_z(k)
 
         ident_f = keep.tile([P, P], F32)
         make_identity(nc, ident_f[:])
@@ -98,66 +105,29 @@ def tile_dynamix_pb_t_e_kernel(tc, z, mlp_out, t2, A, W_words, W_scales, h, out)
             out=floor[:], in0=relu_flag[:], scalar1=BF16_MAX, scalar2=-BF16_MAX, op0=ALU.mult, op1=ALU.add
         )
 
-        t2_f = keep.tile([P, 1], F32)
-        nc.vector.tensor_copy(out=t2_f[:], in_=t2_sb[:])
-        inv_t2 = keep.tile([P, 1], F32)
-        nc.vector.reciprocal(out=inv_t2[:], in_=t2_f[:])
-        logit = keep.tile([P, N_TILES, E], F32)
-        nc.vector.tensor_scalar(
-            out=logit[:], in0=mlp_sb[:], scalar1=inv_t2[:, 0:1], scalar2=-1.0, op0=ALU.mult, op1=ALU.mult
-        )
-        top = keep.tile([P, N_TILES], F32)
-        nc.vector.tensor_reduce(out=top[:], in_=logit[:], axis=AX.X, op=ALU.max)
-        nc.vector.tensor_tensor(
-            out=logit[:], in0=logit[:], in1=top[:].unsqueeze(2).to_broadcast([P, N_TILES, E]), op=ALU.subtract
-        )
-        expd = keep.tile([P, N_TILES, E], F32)
-        nc.scalar.activation(out=expd[:], in_=logit[:], func=ACT.Exp)
-        total = keep.tile([P, N_TILES], F32)
-        nc.vector.tensor_reduce(out=total[:], in_=expd[:], axis=AX.X, op=ALU.add)
-        inv_total = keep.tile([P, N_TILES], F32)
-        nc.vector.reciprocal(out=inv_total[:], in_=total[:])
-        gate = keep.tile([P, N_TILES, E], F32)
-        nc.vector.tensor_tensor(
-            out=gate[:], in0=expd[:], in1=inv_total[:].unsqueeze(2).to_broadcast([P, N_TILES, E]), op=ALU.mult
-        )
-
-        rest = gate
-        for i in range(PIECES):
-            piece = gate_pad[:, :, E * i : E * (i + 1)]
-            nc.vector.tensor_copy(out=piece, in_=rest[:])
-            if i + 1 < PIECES:
-                smaller = keep.tile([P, N_TILES, E], F32, name="rest%d" % i)
-                nc.vector.tensor_tensor(out=smaller[:], in0=rest[:], in1=piece, op=ALU.subtract)
-                rest = smaller
-        a_stat = keep.tile([P, PACK, P], BF16)
-        h_stat = keep.tile([P, PACK, P], BF16)
-        nc.vector.tensor_copy(out=a_stat[:], in_=a_rows[:].rearrange("j (q t) -> j t q", t=PACK))
-        nc.vector.tensor_copy(out=h_stat[:], in_=h_rows[:].rearrange("j (q t) -> j t q", t=PACK))
-        gate_rows = keep.tile([P, B], BF16)
-        for first in range(0, N_TILES, TILES_PER_BANK):
-            rows_ps = psum_g.tile([P, TILES_PER_BANK * P], BF16, tag="g_ps")
-            for j in range(TILES_PER_BANK):
-                nc.tensor.transpose(rows_ps[:, P * j : P * (j + 1)], gate_pad[:, first + j, :], ident_b[:])
-            nc.scalar.copy(out=gate_rows[:, P * first : P * (first + TILES_PER_BANK)], in_=rows_ps[:])
-
         z_codes = keep.tile([P, B], U32, align_bytes=64)
         z_scales = keep.tile([P, B], U8, align_bytes=64)
-        out_sb = keep.tile([P, PACK, B], F32)
+        gate_rows = keep.tile([P, B], BF16)
+        out_sb = {}
         grouped = {}
         leaves = {}
         mixed = {}
         h_tiles = {}
         back = {}
+        h_pairs = {}
+        mixed_a_ps = {}
 
         def tile_cols(c):
             return slice(c * P, (c + 1) * P)
 
+        def cols_in_chunk(c):
+            return slice((c % TILES_PER_CHUNK) * P, (c % TILES_PER_CHUNK + 1) * P)
+
         def regroup(c):
             grouped[c] = work.tile([P, P, PACK], BF16, align_bytes=64, name="grouped")
             nc.vector.tensor_scalar(
-                out=grouped[c][:],
-                in0=z_raw[:, :, tile_cols(c)].rearrange("q t b -> q b t"),
+                out=grouped[c][:].rearrange("q (n i) t -> q n t i", i=RUN),
+                in0=z_raw[c // TILES_PER_CHUNK][:, :, cols_in_chunk(c)].rearrange("q t (n i) -> q n t i", i=RUN),
                 scalar1=floor[:, 0:1],
                 scalar2=None,
                 op0=ALU.max,
@@ -170,16 +140,34 @@ def tile_dynamix_pb_t_e_kernel(tc, z, mlp_out, t2, A, W_words, W_scales, h, out)
                 in_=grouped[c][:].rearrange("q b t -> q (b t)"),
             )
 
+        def build_gate_rows(first):
+            rows_ps = psum_g.tile([P, TILES_PER_BANK * P], BF16, tag="g_ps")
+            for j in range(TILES_PER_BANK):
+                nc.tensor.transpose(rows_ps[:, P * j : P * (j + 1)], gate_pad[:, first + j, :], ident_b[:])
+            nc.scalar.copy(out=gate_rows[:, P * first : P * (first + TILES_PER_BANK)], in_=rows_ps[:])
+
+        def chunk_cols(i):
+            return slice((i // PACK) * CHUNK, (i // PACK + 1) * CHUNK)
+
+        def mixed_a(i):
+            mixed_a_ps[i] = psum_g.tile([P, CHUNK], F32, tag="g_ps", name="g_ps")
+            nc.tensor.matmul(
+                out=mixed_a_ps[i][:], lhsT=a_stat[:, i % PACK, :], rhs=gate_rows[:, chunk_cols(i)], start=True, stop=True
+            )
+
         def a_term(i):
-            t = i % PACK
-            cols = slice((i // PACK) * CHUNK, (i // PACK + 1) * CHUNK)
-            g_ps = psum_g.tile([P, CHUNK], F32, tag="g_ps")
-            nc.tensor.matmul(out=g_ps[:], lhsT=a_stat[:, t, :], rhs=gate_rows[:, cols], start=True, stop=True)
-            nc.vector.tensor_tensor(out=out_sb[:, t, cols], in0=g_ps[:], in1=z_raw[:, t, cols], op=ALU.mult)
+            if i % PACK == 0:
+                out_sb[i // PACK] = out_pool.tile([P, PACK, CHUNK], F32, name="out_chunk")
+            nc.vector.tensor_tensor(
+                out=out_sb[i // PACK][:, i % PACK, :],
+                in0=mixed_a_ps[i][:],
+                in1=z_raw[i // PACK][:, i % PACK, :],
+                op=ALU.mult,
+            )
 
         def experts(c):
-            leaves[c] = []
-            for e in range(E):
+            leaves[c] = {}
+            for e in (0, 2, 1, 3):
                 p_ps = psum_p.tile([P, M], F32, name="p_ps%d" % e)
                 nc.tensor.matmul_mx(
                     out=p_ps[:],
@@ -190,7 +178,7 @@ def tile_dynamix_pb_t_e_kernel(tc, z, mlp_out, t2, A, W_words, W_scales, h, out)
                     start=True,
                     stop=True,
                 )
-                leaves[c].append(p_ps[:].rearrange("b (q t) -> b t q", t=PACK))
+                leaves[c][e] = p_ps[:].rearrange("b (q t) -> b t q", t=PACK)
 
         def mix(c):
             s0 = work.tile([P, PACK, P], F32)
@@ -220,6 +208,13 @@ def tile_dynamix_pb_t_e_kernel(tc, z, mlp_out, t2, A, W_words, W_scales, h, out)
                 )
                 h_tiles[c].append(gh)
 
+        def pair_h(c):
+            h_pairs[c] = []
+            for e in range(0, E, 2):
+                pair = work.tile([P, PACK - PLAIN_H_GROUPS, P], F32, name="pair%d" % e)
+                nc.gpsimd.tensor_tensor(out=pair[:], in0=h_tiles[c][e][:], in1=h_tiles[c][e + 1][:], op=ALU.add)
+                h_pairs[c].append(pair)
+
         def turn_back(c):
             back[c] = psum_f.tile([P, PACK, P], F32, name="f_ps")
             for t in range(PACK):
@@ -231,44 +226,85 @@ def tile_dynamix_pb_t_e_kernel(tc, z, mlp_out, t2, A, W_words, W_scales, h, out)
                         out=back[c][:, t, :], lhsT=h_stat[:, t, :], rhs=gate_rows[:, tile_cols(c)], start=False, stop=True
                     )
                 else:
-                    for e in range(E):
+                    for i in range(len(h_pairs[c])):
                         nc.tensor.matmul(
                             out=back[c][:, t, :],
-                            lhsT=h_tiles[c][e][:, t - PLAIN_H_GROUPS, :],
+                            lhsT=h_pairs[c][i][:, t - PLAIN_H_GROUPS, :],
                             rhs=ident_f[:],
                             start=False,
-                            stop=(e == E - 1),
+                            stop=(i == len(h_pairs[c]) - 1),
                             is_transpose=True,
                         )
 
         def finish(c):
-            nc.vector.tensor_tensor(
-                out=out_sb[:, :, tile_cols(c)], in0=back[c][:], in1=out_sb[:, :, tile_cols(c)], op=ALU.add
-            )
+            k = c // TILES_PER_CHUNK
+            part = out_sb[k][:, :, cols_in_chunk(c)]
+            nc.vector.tensor_tensor(out=part, in0=back[c][:], in1=part, op=ALU.add)
             if c % TILES_PER_CHUNK == TILES_PER_CHUNK - 1:
-                cols = slice((c + 1) * P - CHUNK, (c + 1) * P)
-                nc.sync.dma_start(out=out_rows[:, :, cols], in_=out_sb[:, :, cols])
+                nc.sync.dma_start(out=out_rows[:, :, k * CHUNK : (k + 1) * CHUNK], in_=out_sb[k][:])
 
+        t2_f = keep.tile([P, 1], F32)
+        nc.vector.tensor_copy(out=t2_f[:], in_=t2_sb[:])
+        inv_t2 = keep.tile([P, 1], F32)
+        nc.vector.reciprocal(out=inv_t2[:], in_=t2_f[:])
+        logit = keep.tile([P, N_TILES, E], F32)
+        nc.vector.tensor_scalar(
+            out=logit[:], in0=mlp_sb[:], scalar1=inv_t2[:, 0:1], scalar2=-1.0, op0=ALU.mult, op1=ALU.mult
+        )
+        top = keep.tile([P, N_TILES], F32)
+        nc.vector.tensor_reduce(out=top[:], in_=logit[:], axis=AX.X, op=ALU.max)
+        nc.vector.tensor_tensor(
+            out=logit[:], in0=logit[:], in1=top[:].unsqueeze(2).to_broadcast([P, N_TILES, E]), op=ALU.subtract
+        )
+        expd = keep.tile([P, N_TILES, E], F32)
+        nc.scalar.activation(out=expd[:], in_=logit[:], func=ACT.Exp)
         regroup(0)
         regroup(1)
         quantise(0)
+        experts(0)
+        total = keep.tile([P, N_TILES], F32)
+        nc.vector.tensor_reduce(out=total[:], in_=expd[:], axis=AX.X, op=ALU.add)
+        inv_total = keep.tile([P, N_TILES], F32)
+        nc.vector.reciprocal(out=inv_total[:], in_=total[:])
+        gate = keep.tile([P, N_TILES, E], F32)
+        nc.vector.tensor_tensor(
+            out=gate[:], in0=expd[:], in1=inv_total[:].unsqueeze(2).to_broadcast([P, N_TILES, E]), op=ALU.mult
+        )
+
         regroup(2)
         quantise(1)
-        gated_h(0)
-        for i in range(PACK):
-            a_term(i)
-        for c in range(N_TILES + 1):
+
+        rest = gate
+        for i in range(PIECES):
+            piece = gate_pad[:, :, E * i : E * (i + 1)]
+            nc.vector.tensor_copy(out=piece, in_=rest[:])
+            if i + 1 < PIECES:
+                smaller = keep.tile([P, N_TILES, E], F32, name="rest%d" % i)
+                nc.vector.tensor_tensor(out=smaller[:], in0=rest[:], in1=piece, op=ALU.subtract)
+                rest = smaller
+        a_stat = keep.tile([P, PACK, P], BF16)
+        h_stat = keep.tile([P, PACK, P], BF16)
+        nc.vector.tensor_copy(out=a_stat[:], in_=a_rows[:].rearrange("j (q t) -> j t q", t=PACK))
+        nc.vector.tensor_copy(out=h_stat[:], in_=h_rows[:].rearrange("j (q t) -> j t q", t=PACK))
+
+        for c in range(N_TILES + 3):
+            if 1 <= c < N_TILES + 1:
+                pair_h(c - 1)
             if c < N_TILES:
-                experts(c)
                 mix(c)
+                if c % TILES_PER_BANK == 0:
+                    build_gate_rows(c)
+                gated_h(c)
+            if 2 <= c < N_TILES + 2:
+                turn_back(c - 2)
+            if c < N_TILES:
+                mixed_a(c)
             if c + 1 < N_TILES:
-                gated_h(c + 1)
-            if c >= 1:
-                turn_back(c - 1)
-            if c + PACK < N_TILES:
-                a_term(c + PACK)
-            if c >= 1:
-                finish(c - 1)
+                experts(c + 1)
+            if c < N_TILES:
+                a_term(c)
+            if c >= 3:
+                finish(c - 3)
             if c + 3 < N_TILES:
                 regroup(c + 3)
             if c + 2 < N_TILES:

@@ -28,6 +28,7 @@ PLAIN_H_GROUPS = 2
 RUN = 4
 TILES_PER_BANK = 8
 BF16_MAX = 3.3895313892515355e38
+BASE = E - 1
 
 FLOPS = 2 * E * M * M * B
 
@@ -56,6 +57,7 @@ def tile_dynamix_pb_t_e_kernel(tc, z, mlp_out, t2, A, W_words, W_scales, h, out)
         w_planes = keep.tile([P, E, M], U8, align_bytes=64)
         gate_pad = keep.tile([P, N_TILES, P], BF16)
         warm = keep.tile([P, 1], F32)
+        h_base_bf = keep.tile([P, PACK], BF16)
 
         nc.vector.memset(w_planes[:].rearrange("p g n -> p (g n)").bitcast(I32), 0)
         nc.vector.memset(a_rows[:], 0.0)
@@ -65,6 +67,7 @@ def tile_dynamix_pb_t_e_kernel(tc, z, mlp_out, t2, A, W_words, W_scales, h, out)
 
         nc.scalar.dma_start(out=mlp_sb[:], in_=mlp_out.rearrange("(c p) e -> p c e", p=P))
         nc.scalar.dma_start(out=t2_sb[:], in_=t2.partition_broadcast(P))
+        nc.scalar.dma_start(out=h_base_bf[:], in_=h[BASE].rearrange("(q t) -> q t", t=PACK))
         nc.scalar.activation(out=warm[:], in_=warm[:], func=ACT.Exp)
 
         for quad in range(4):
@@ -198,22 +201,15 @@ def tile_dynamix_pb_t_e_kernel(tc, z, mlp_out, t2, A, W_words, W_scales, h, out)
 
         def gated_h(c):
             h_tiles[c] = []
-            for e in range(E):
+            for e in range(BASE):
                 gh = work.tile([P, PACK - PLAIN_H_GROUPS, P], F32, name="gh%d" % e)
-                nc.scalar.activation(
-                    out=gh[:],
-                    in_=h_all[:, e, :].rearrange("b (q t) -> b t q", t=PACK)[:, PLAIN_H_GROUPS:PACK, :],
-                    func=ACT.Copy,
-                    scale=gate[:, c, e : e + 1],
-                )
+                nc.scalar.activation(out=gh[:], in_=h_diff[:, e, :, :], func=ACT.Copy, scale=gate[:, c, e : e + 1])
                 h_tiles[c].append(gh)
 
         def pair_h(c):
-            h_pairs[c] = []
-            for e in range(0, E, 2):
-                pair = work.tile([P, PACK - PLAIN_H_GROUPS, P], F32, name="pair%d" % e)
-                nc.gpsimd.tensor_tensor(out=pair[:], in0=h_tiles[c][e][:], in1=h_tiles[c][e + 1][:], op=ALU.add)
-                h_pairs[c].append(pair)
+            pair = work.tile([P, PACK - PLAIN_H_GROUPS, P], F32, name="pair")
+            nc.gpsimd.tensor_tensor(out=pair[:], in0=h_tiles[c][0][:], in1=h_tiles[c][1][:], op=ALU.add)
+            h_pairs[c] = [pair, h_tiles[c][2]]
 
         def turn_back(c):
             back[c] = psum_f.tile([P, PACK, P], F32, name="f_ps")
@@ -238,8 +234,13 @@ def tile_dynamix_pb_t_e_kernel(tc, z, mlp_out, t2, A, W_words, W_scales, h, out)
 
         def finish(c):
             k = c // TILES_PER_CHUNK
-            part = out_sb[k][:, :, cols_in_chunk(c)]
-            nc.vector.tensor_tensor(out=part, in0=back[c][:], in1=part, op=ALU.add)
+            part = out_sb[k][:, 0:PLAIN_H_GROUPS, cols_in_chunk(c)]
+            nc.vector.tensor_tensor(out=part, in0=back[c][:, 0:PLAIN_H_GROUPS, :], in1=part, op=ALU.add)
+            for t in range(PLAIN_H_GROUPS, PACK):
+                part = out_sb[k][:, t, cols_in_chunk(c)]
+                nc.vector.scalar_tensor_tensor(
+                    out=part, in0=back[c][:, t, :], scalar=h_base[:, t : t + 1], in1=part, op0=ALU.add, op1=ALU.add
+                )
             if c % TILES_PER_CHUNK == TILES_PER_CHUNK - 1:
                 nc.sync.dma_start(out=out_rows[:, :, k * CHUNK : (k + 1) * CHUNK], in_=out_sb[k][:])
 
@@ -286,6 +287,15 @@ def tile_dynamix_pb_t_e_kernel(tc, z, mlp_out, t2, A, W_words, W_scales, h, out)
         h_stat = keep.tile([P, PACK, P], BF16)
         nc.vector.tensor_copy(out=a_stat[:], in_=a_rows[:].rearrange("j (q t) -> j t q", t=PACK))
         nc.vector.tensor_copy(out=h_stat[:], in_=h_rows[:].rearrange("j (q t) -> j t q", t=PACK))
+
+        def engine_groups(e):
+            return h_all[:, e, :].rearrange("b (q t) -> b t q", t=PACK)[:, PLAIN_H_GROUPS:PACK, :]
+
+        h_diff = keep.tile([P, BASE, PACK - PLAIN_H_GROUPS, P], F32)
+        for e in range(BASE):
+            nc.vector.tensor_tensor(out=h_diff[:, e, :, :], in0=engine_groups(e), in1=engine_groups(BASE), op=ALU.subtract)
+        h_base = keep.tile([P, PACK], F32)
+        nc.vector.tensor_copy(out=h_base[:], in_=h_base_bf[:])
 
         for c in range(N_TILES + 3):
             if 1 <= c < N_TILES + 1:

@@ -215,22 +215,26 @@ def tile_dynamix_pb_t_e_kernel(tc, z, mlp_out, t2, A, W_words, W_scales, h, out)
             back[c] = psum_f.tile([P, PACK, P], F32, name="f_ps")
             for t in range(PACK):
                 nc.tensor.matmul(
-                    out=back[c][:, t, :], lhsT=mixed[c][:, t, :], rhs=ident_f[:], start=True, stop=False, is_transpose=True
+                    out=back[c][:, t, :], lhsT=mixed[c][:, t, :], rhs=ident_f[:], start=(t == 0), stop=False, is_transpose=True
                 )
-                if t < PLAIN_H_GROUPS:
+            for part in h_pairs[c]:
+                for t in range(PLAIN_H_GROUPS, PACK):
                     nc.tensor.matmul(
-                        out=back[c][:, t, :], lhsT=h_stat[:, t, :], rhs=gate_rows[:, tile_cols(c)], start=False, stop=True
+                        out=back[c][:, t, :],
+                        lhsT=part[:, t - PLAIN_H_GROUPS, :],
+                        rhs=ident_f[:],
+                        start=False,
+                        stop=False,
+                        is_transpose=True,
                     )
-                else:
-                    for i in range(len(h_pairs[c])):
-                        nc.tensor.matmul(
-                            out=back[c][:, t, :],
-                            lhsT=h_pairs[c][i][:, t - PLAIN_H_GROUPS, :],
-                            rhs=ident_f[:],
-                            start=False,
-                            stop=(i == len(h_pairs[c]) - 1),
-                            is_transpose=True,
-                        )
+            for t in range(PLAIN_H_GROUPS):
+                nc.tensor.matmul(
+                    out=back[c][:, t, :],
+                    lhsT=h_stat[:, t, :],
+                    rhs=gate_rows[:, tile_cols(c)],
+                    start=False,
+                    stop=(t == PLAIN_H_GROUPS - 1),
+                )
 
         def finish(c):
             k = c // TILES_PER_CHUNK

@@ -28,6 +28,7 @@ PLAIN_H_GROUPS = 2
 RUN = 4
 TILES_PER_BANK = 8
 BF16_MAX = 3.3895313892515355e38
+SCALAR_GROUPS = 2
 BASE = E - 1
 
 FLOPS = 2 * E * M * M * B
@@ -115,6 +116,7 @@ def tile_dynamix_pb_t_e_kernel(tc, z, mlp_out, t2, A, W_words, W_scales, h, out)
         grouped = {}
         leaves = {}
         mixed = {}
+        scaled = {}
         h_tiles = {}
         back = {}
         h_pairs = {}
@@ -183,21 +185,41 @@ def tile_dynamix_pb_t_e_kernel(tc, z, mlp_out, t2, A, W_words, W_scales, h, out)
                 )
                 leaves[c][e] = p_ps[:].rearrange("b (q t) -> b t q", t=PACK)
 
-        def mix(c):
+        def mix_scalar(c):
             s0 = work.tile([P, PACK, P], F32)
             s2 = work.tile([P, PACK, P], F32)
-            s01 = work.tile([P, PACK, P], F32)
-            s23 = work.tile([P, PACK, P], F32)
-            mixed[c] = work.tile([P, PACK, P], F32, name="mixed")
+            s3 = work.tile([P, SCALAR_GROUPS, P], F32)
             nc.scalar.activation(out=s0[:], in_=leaves[c][0], func=ACT.Copy, scale=gate[:, c, 0:1])
             nc.scalar.activation(out=s2[:], in_=leaves[c][2], func=ACT.Copy, scale=gate[:, c, 2:3])
+            nc.scalar.activation(out=s3[:], in_=leaves[c][3][:, 0:SCALAR_GROUPS, :], func=ACT.Copy, scale=gate[:, c, 3:4])
+            scaled[c] = (s0, s2, s3)
+
+        def mix_first(c):
+            s01 = work.tile([P, PACK, P], F32)
             nc.vector.scalar_tensor_tensor(
-                out=s01[:], in0=leaves[c][1], scalar=gate[:, c, 1:2], in1=s0[:], op0=ALU.mult, op1=ALU.add
+                out=s01[:], in0=leaves[c][1], scalar=gate[:, c, 1:2], in1=scaled[c][0][:], op0=ALU.mult, op1=ALU.add
             )
+            s23_low = work.tile([P, SCALAR_GROUPS, P], F32)
+            nc.gpsimd.tensor_tensor(
+                out=s23_low[:], in0=scaled[c][1][:, 0:SCALAR_GROUPS, :], in1=scaled[c][2][:], op=ALU.add
+            )
+            mixed[c] = [s01, s23_low]
+
+        def mix_second(c):
+            s23_high = work.tile([P, PACK - SCALAR_GROUPS, P], F32)
             nc.vector.scalar_tensor_tensor(
-                out=s23[:], in0=leaves[c][3], scalar=gate[:, c, 3:4], in1=s2[:], op0=ALU.mult, op1=ALU.add
+                out=s23_high[:],
+                in0=leaves[c][3][:, SCALAR_GROUPS:PACK, :],
+                scalar=gate[:, c, 3:4],
+                in1=scaled[c][1][:, SCALAR_GROUPS:PACK, :],
+                op0=ALU.mult,
+                op1=ALU.add,
             )
-            nc.gpsimd.tensor_tensor(out=mixed[c][:], in0=s01[:], in1=s23[:], op=ALU.add)
+            all_high = work.tile([P, PACK - SCALAR_GROUPS, P], F32)
+            nc.gpsimd.tensor_tensor(
+                out=all_high[:], in0=mixed[c][0][:, SCALAR_GROUPS:PACK, :], in1=s23_high[:], op=ALU.add
+            )
+            mixed[c].append(all_high)
 
         def gated_h(c):
             h_tiles[c] = []
@@ -213,9 +235,19 @@ def tile_dynamix_pb_t_e_kernel(tc, z, mlp_out, t2, A, W_words, W_scales, h, out)
 
         def turn_back(c):
             back[c] = psum_f.tile([P, PACK, P], F32, name="f_ps")
+            s01, s23_low, all_high = mixed[c]
             for t in range(PACK):
                 nc.tensor.matmul(
-                    out=back[c][:, t, :], lhsT=mixed[c][:, t, :], rhs=ident_f[:], start=(t == 0), stop=False, is_transpose=True
+                    out=back[c][:, t, :],
+                    lhsT=s01[:, t, :] if t < SCALAR_GROUPS else all_high[:, t - SCALAR_GROUPS, :],
+                    rhs=ident_f[:],
+                    start=(t == 0),
+                    stop=False,
+                    is_transpose=True,
+                )
+            for t in range(SCALAR_GROUPS):
+                nc.tensor.matmul(
+                    out=back[c][:, t, :], lhsT=s23_low[:, t, :], rhs=ident_f[:], start=False, stop=False, is_transpose=True
                 )
             for part in h_pairs[c]:
                 for t in range(PLAIN_H_GROUPS, PACK):
@@ -305,20 +337,22 @@ def tile_dynamix_pb_t_e_kernel(tc, z, mlp_out, t2, A, W_words, W_scales, h, out)
             if 1 <= c < N_TILES + 1:
                 pair_h(c - 1)
             if c < N_TILES:
-                mix(c)
-                if c % TILES_PER_BANK == 0:
-                    build_gate_rows(c)
+                mix_scalar(c)
+                mix_first(c)
                 gated_h(c)
-            if 2 <= c < N_TILES + 2:
-                turn_back(c - 2)
-            if c < N_TILES:
-                mixed_a(c)
-            if c + 1 < N_TILES:
-                experts(c + 1)
-            if c < N_TILES:
-                a_term(c)
             if c >= 3:
                 finish(c - 3)
+            if c < N_TILES:
+                mix_second(c)
+            if 2 <= c < N_TILES + 2:
+                turn_back(c - 2)
+            for i in range(0 if c == 0 else c + 1, min(c + 2, N_TILES)):
+                if i % TILES_PER_BANK == 0:
+                    build_gate_rows(i)
+                mixed_a(i)
+                a_term(i)
+            if c + 1 < N_TILES:
+                experts(c + 1)
             if c + 3 < N_TILES:
                 regroup(c + 3)
             if c + 2 < N_TILES:

@@ -28,7 +28,7 @@ PLAIN_H_GROUPS = 2
 RUN = 4
 TILES_PER_BANK = 8
 BF16_MAX = 3.3895313892515355e38
-SCALAR_GROUPS = 2
+SCALAR_GROUPS = 3
 BASE = E - 1
 
 FLOPS = 2 * E * M * M * B
@@ -277,7 +277,9 @@ def tile_dynamix_pb_t_e_kernel(tc, z, mlp_out, t2, A, W_words, W_scales, h, out)
                 nc.vector.scalar_tensor_tensor(
                     out=part, in0=back[c][:, t, :], scalar=h_base[:, t : t + 1], in1=part, op0=ALU.add, op1=ALU.add
                 )
-            if c % TILES_PER_CHUNK == TILES_PER_CHUNK - 1:
+            if k == N_CHUNKS - 1:
+                nc.sync.dma_start(out=out_rows[:, :, tile_cols(c)], in_=out_sb[k][:, :, cols_in_chunk(c)])
+            elif c % TILES_PER_CHUNK == TILES_PER_CHUNK - 1:
                 nc.sync.dma_start(out=out_rows[:, :, k * CHUNK : (k + 1) * CHUNK], in_=out_sb[k][:])
 
         t2_f = keep.tile([P, 1], F32)

@@ -28,6 +28,8 @@ PLAIN_H_GROUPS = 2
 RUN = 4
 TILES_PER_BANK = 8
 BF16_MAX = 3.3895313892515355e38
+EXTRA_PERIOD = 8
+EXTRA_TILES = 3
 SCALAR_GROUPS = 3
 BASE = E - 1
 
@@ -221,15 +223,23 @@ def tile_dynamix_pb_t_e_kernel(tc, z, mlp_out, t2, A, W_words, W_scales, h, out)
             )
             mixed[c].append(all_high)
 
+        def plain_groups(c):
+            return PLAIN_H_GROUPS + (1 if c % EXTRA_PERIOD < EXTRA_TILES else 0)
+
         def gated_h(c):
             h_tiles[c] = []
             for e in range(BASE):
-                gh = work.tile([P, PACK - PLAIN_H_GROUPS, P], F32, name="gh%d" % e)
-                nc.scalar.activation(out=gh[:], in_=h_diff[:, e, :, :], func=ACT.Copy, scale=gate[:, c, e : e + 1])
+                gh = work.tile([P, PACK - plain_groups(c), P], F32, name="gh%d" % e)
+                nc.scalar.activation(
+                    out=gh[:],
+                    in_=h_diff[:, e, plain_groups(c) - PLAIN_H_GROUPS :, :],
+                    func=ACT.Copy,
+                    scale=gate[:, c, e : e + 1],
+                )
                 h_tiles[c].append(gh)
 
         def pair_h(c):
-            pair = work.tile([P, PACK - PLAIN_H_GROUPS, P], F32, name="pair")
+            pair = work.tile([P, PACK - plain_groups(c), P], F32, name="pair")
             nc.gpsimd.tensor_tensor(out=pair[:], in0=h_tiles[c][0][:], in1=h_tiles[c][1][:], op=ALU.add)
             h_pairs[c] = [pair, h_tiles[c][2]]
 
@@ -250,29 +260,29 @@ def tile_dynamix_pb_t_e_kernel(tc, z, mlp_out, t2, A, W_words, W_scales, h, out)
                     out=back[c][:, t, :], lhsT=s23_low[:, t, :], rhs=ident_f[:], start=False, stop=False, is_transpose=True
                 )
             for part in h_pairs[c]:
-                for t in range(PLAIN_H_GROUPS, PACK):
+                for t in range(plain_groups(c), PACK):
                     nc.tensor.matmul(
                         out=back[c][:, t, :],
-                        lhsT=part[:, t - PLAIN_H_GROUPS, :],
+                        lhsT=part[:, t - plain_groups(c), :],
                         rhs=ident_f[:],
                         start=False,
                         stop=False,
                         is_transpose=True,
                     )
-            for t in range(PLAIN_H_GROUPS):
+            for t in range(plain_groups(c)):
                 nc.tensor.matmul(
                     out=back[c][:, t, :],
                     lhsT=h_stat[:, t, :],
                     rhs=gate_rows[:, tile_cols(c)],
                     start=False,
-                    stop=(t == PLAIN_H_GROUPS - 1),
+                    stop=(t == plain_groups(c) - 1),
                 )
 
         def finish(c):
             k = c // TILES_PER_CHUNK
-            part = out_sb[k][:, 0:PLAIN_H_GROUPS, cols_in_chunk(c)]
-            nc.vector.tensor_tensor(out=part, in0=back[c][:, 0:PLAIN_H_GROUPS, :], in1=part, op=ALU.add)
-            for t in range(PLAIN_H_GROUPS, PACK):
+            part = out_sb[k][:, 0 : plain_groups(c), cols_in_chunk(c)]
+            nc.vector.tensor_tensor(out=part, in0=back[c][:, 0 : plain_groups(c), :], in1=part, op=ALU.add)
+            for t in range(plain_groups(c), PACK):
                 part = out_sb[k][:, t, cols_in_chunk(c)]
                 nc.vector.scalar_tensor_tensor(
                     out=part, in0=back[c][:, t, :], scalar=h_base[:, t : t + 1], in1=part, op0=ALU.add, op1=ALU.add

@@ -31,6 +31,7 @@ BF16_MAX = 3.3895313892515355e38
 EXTRA_PERIOD = 8
 EXTRA_TILES = 3
 SCALAR_GROUPS = 3
+ROWS_AHEAD = 4
 BASE = E - 1
 
 FLOPS = 2 * E * M * M * B
@@ -359,8 +360,10 @@ def tile_dynamix_pb_t_e_kernel(tc, z, mlp_out, t2, A, W_words, W_scales, h, out)
             if 2 <= c < N_TILES + 2:
                 turn_back(c - 2)
             for i in range(0 if c == 0 else c + 1, min(c + 2, N_TILES)):
-                if i % TILES_PER_BANK == 0:
-                    build_gate_rows(i)
+                if i == 0:
+                    build_gate_rows(0)
+                if i % TILES_PER_BANK == ROWS_AHEAD and i + ROWS_AHEAD < N_TILES:
+                    build_gate_rows(i + ROWS_AHEAD)
                 mixed_a(i)
                 a_term(i)
             if c + 1 < N_TILES:

@@ -357,17 +357,20 @@ def tile_dynamix_pb_t_e_kernel(tc, z, mlp_out, t2, A, W_words, W_scales, h, out)
                 finish(c - 3)
             if c < N_TILES:
                 mix_second(c)
+            if (c + 2) % TILES_PER_BANK == ROWS_AHEAD and c + 2 + ROWS_AHEAD < N_TILES:
+                build_gate_rows(c + 2 + ROWS_AHEAD)
             if 2 <= c < N_TILES + 2:
                 turn_back(c - 2)
-            for i in range(0 if c == 0 else c + 1, min(c + 2, N_TILES)):
-                if i == 0:
-                    build_gate_rows(0)
-                if i % TILES_PER_BANK == ROWS_AHEAD and i + ROWS_AHEAD < N_TILES:
-                    build_gate_rows(i + ROWS_AHEAD)
-                mixed_a(i)
-                a_term(i)
+            if c == 0:
+                build_gate_rows(0)
+                mixed_a(0)
+                a_term(0)
+                mixed_a(1)
             if c + 1 < N_TILES:
+                a_term(c + 1)
                 experts(c + 1)
+            if c + 2 < N_TILES:
+                mixed_a(c + 2)
             if c + 3 < N_TILES:
                 regroup(c + 3)
             if c + 2 < N_TILES:

@@ -52,7 +52,7 @@ def tile_dynamix_pb_t_e_kernel(tc, z, mlp_out, t2, A, W_words, W_scales, h, out)
         z_rows = z.rearrange("(q t) b -> q t b", t=PACK)
         out_rows = out.rearrange("(q t) b -> q t b", t=PACK)
 
-        mlp_sb = keep.tile([P, N_TILES, E], BF16)
+        logit_rows = keep.tile([P, P * E], BF16)
         t2_sb = keep.tile([P, 1], BF16)
         a_rows = keep.tile([P, M], BF16)
         h_rows = keep.tile([P, M], BF16)
@@ -64,13 +64,15 @@ def tile_dynamix_pb_t_e_kernel(tc, z, mlp_out, t2, A, W_words, W_scales, h, out)
         h_base_bf = keep.tile([P, PACK], BF16)
 
         nc.vector.memset(w_planes[:].rearrange("p g n -> p (g n)").bitcast(I32), 0)
+        nc.gpsimd.memset(logit_rows[N_TILES : 2 * N_TILES, :], 0.0)
+        nc.gpsimd.memset(logit_rows[2 * N_TILES : P, :], 0.0)
         nc.vector.memset(a_rows[:], 0.0)
         nc.vector.memset(h_rows[:], 0.0)
         nc.vector.memset(warm[:], 0.0)
         nc.vector.memset(gate_pad[:].rearrange("p c j -> p (c j)").bitcast(I32), 0)
 
-        nc.scalar.dma_start(out=mlp_sb[:], in_=mlp_out.rearrange("(c p) e -> p c e", p=P))
         nc.scalar.dma_start(out=t2_sb[:], in_=t2.partition_broadcast(P))
+        nc.scalar.dma_start(out=logit_rows[0:N_TILES, :], in_=mlp_out.rearrange("(c p) e -> c (p e)", p=P))
         nc.scalar.dma_start(out=h_base_bf[:], in_=h[BASE].rearrange("(q t) -> q t", t=PACK))
         nc.scalar.activation(out=warm[:], in_=warm[:], func=ACT.Exp)
 
@@ -297,9 +299,17 @@ def tile_dynamix_pb_t_e_kernel(tc, z, mlp_out, t2, A, W_words, W_scales, h, out)
         nc.vector.tensor_copy(out=t2_f[:], in_=t2_sb[:])
         inv_t2 = keep.tile([P, 1], F32)
         nc.vector.reciprocal(out=inv_t2[:], in_=t2_f[:])
+        logit_ps = psum_g.tile([P, E, P], BF16, tag="g_ps")
+        for e in range(E):
+            nc.tensor.transpose(logit_ps[:, e, :], logit_rows[:].rearrange("c (p e) -> c e p", e=E)[:, e, :], ident_b[:])
         logit = keep.tile([P, N_TILES, E], F32)
         nc.vector.tensor_scalar(
-            out=logit[:], in0=mlp_sb[:], scalar1=inv_t2[:, 0:1], scalar2=-1.0, op0=ALU.mult, op1=ALU.mult
+            out=logit[:],
+            in0=logit_ps[:, :, 0:N_TILES].rearrange("p e c -> p c e"),
+            scalar1=inv_t2[:, 0:1],
+            scalar2=-1.0,
+            op0=ALU.mult,
+            op1=ALU.mult,
         )
         top = keep.tile([P, N_TILES], F32)
         nc.vector.tensor_reduce(out=top[:], in_=logit[:], axis=AX.X, op=ALU.max)

@@ -134,10 +134,11 @@ def tile_dynamix_pb_t_e_kernel(tc, z, mlp_out, t2, A, W_words, W_scales, h, out)
             return slice((c % TILES_PER_CHUNK) * P, (c % TILES_PER_CHUNK + 1) * P)
 
         def regroup(c):
-            grouped[c] = work.tile([P, P, PACK], BF16, align_bytes=64, name="grouped")
+            first = (c % TILES_PER_CHUNK) * P
+            grouped[c] = work.tile([P, 2 * P, PACK], BF16, align_bytes=64, name="grouped")
             nc.vector.tensor_scalar(
                 out=grouped[c][:].rearrange("q (n i) t -> q n t i", i=RUN),
-                in0=z_raw[c // TILES_PER_CHUNK][:, :, cols_in_chunk(c)].rearrange("q t (n i) -> q n t i", i=RUN),
+                in0=z_raw[c // TILES_PER_CHUNK][:, :, first : first + 2 * P].rearrange("q t (n i) -> q n t i", i=RUN),
                 scalar1=floor[:, 0:1],
                 scalar2=None,
                 op0=ALU.max,
@@ -145,8 +146,8 @@ def tile_dynamix_pb_t_e_kernel(tc, z, mlp_out, t2, A, W_words, W_scales, h, out)
 
         def quantise(c):
             nc.vector.quantize_mx(
-                out=z_codes[:, tile_cols(c)].bitcast(FP8X4),
-                scales=z_scales[:, tile_cols(c)],
+                out=z_codes[:, c * P : (c + 2) * P].bitcast(FP8X4),
+                scales=z_scales[:, c * P : (c + 2) * P],
                 in_=grouped[c][:].rearrange("q b t -> q (b t)"),
             )
 
@@ -319,11 +320,10 @@ def tile_dynamix_pb_t_e_kernel(tc, z, mlp_out, t2, A, W_words, W_scales, h, out)
         expd = keep.tile([P, N_TILES, E], F32)
         nc.scalar.activation(out=expd[:], in_=logit[:], func=ACT.Exp)
         regroup(0)
-        regroup(1)
-        quantise(0)
-        experts(0)
         total = keep.tile([P, N_TILES], F32)
         nc.vector.tensor_reduce(out=total[:], in_=expd[:], axis=AX.X, op=ALU.add)
+        quantise(0)
+        experts(0)
         inv_total = keep.tile([P, N_TILES], F32)
         nc.vector.reciprocal(out=inv_total[:], in_=total[:])
         gate = keep.tile([P, N_TILES, E], F32)
@@ -332,7 +332,6 @@ def tile_dynamix_pb_t_e_kernel(tc, z, mlp_out, t2, A, W_words, W_scales, h, out)
         )
 
         regroup(2)
-        quantise(1)
 
         rest = gate
         for i in range(PIECES):
@@ -381,7 +380,7 @@ def tile_dynamix_pb_t_e_kernel(tc, z, mlp_out, t2, A, W_words, W_scales, h, out)
                 experts(c + 1)
             if c + 2 < N_TILES:
                 mixed_a(c + 2)
-            if c + 3 < N_TILES:
-                regroup(c + 3)
-            if c + 2 < N_TILES:
+            if c % 2 == 0 and c + 2 < N_TILES:
                 quantise(c + 2)
+            if c % 2 == 1 and c + 3 < N_TILES:
+                regroup(c + 3)

from contextlib import ExitStack

import concourse.mybir as mybir
from concourse.masks import make_identity

F32 = mybir.dt.float32
BF16 = mybir.dt.bfloat16
I32 = mybir.dt.int32
U32 = mybir.dt.uint32
U8 = mybir.dt.uint8
FP8X4 = mybir.dt.float8_e4m3fn_x4
ALU = mybir.AluOpType
ACT = mybir.ActivationFunctionType
AX = mybir.AxisListType

P = 128
PACK = 4
E = 4
M = 512
B = 4096
RELU_ROWS = 32
N_TILES = B // P
CHUNK = 512
N_CHUNKS = B // CHUNK
TILES_PER_CHUNK = CHUNK // P
PIECES = 3
PLAIN_H_GROUPS = 2
RUN = 4
TILES_PER_BANK = 8
BF16_MAX = 3.3895313892515355e38
EXTRA_PERIOD = 8
EXTRA_TILES = 3
SCALAR_GROUPS = 3
ROWS_AHEAD = 4
BASE = E - 1

FLOPS = 2 * E * M * M * B


def tile_dynamix_pb_t_e_kernel(tc, z, mlp_out, t2, A, W_words, W_scales, h, out):
    nc = tc.nc
    with ExitStack() as ctx:
        ctx.enter_context(tc.manual_schedule())
        keep = ctx.enter_context(tc.tile_pool(name="keep", bufs=1))
        work = ctx.enter_context(tc.tile_pool(name="work", bufs=3))
        z_pool = ctx.enter_context(tc.tile_pool(name="z_pool", bufs=N_CHUNKS))
        out_pool = ctx.enter_context(tc.tile_pool(name="out_pool", bufs=3))
        psum_p = ctx.enter_context(tc.psum_pool(name="psum_p", bufs=1))
        psum_g = ctx.enter_context(tc.psum_pool(name="psum_g", bufs=2))
        psum_f = ctx.enter_context(tc.psum_pool(name="psum_f", bufs=2))

        z_rows = z.rearrange("(q t) b -> q t b", t=PACK)
        out_rows = out.rearrange("(q t) b -> q t b", t=PACK)

        logit_rows = keep.tile([P, P * E], BF16)
        t2_sb = keep.tile([P, 1], BF16)
        a_rows = keep.tile([P, M], BF16)
        h_rows = keep.tile([P, M], BF16)
        h_all = keep.tile([P, E, M], BF16)
        w_words = keep.tile([P, E, M], U32, align_bytes=64)
        w_planes = keep.tile([P, E, M], U8, align_bytes=64)
        gate_pad = keep.tile([P, N_TILES, P], BF16)
        warm = keep.tile([P, 1], F32)
        h_base_bf = keep.tile([P, PACK], BF16)

        nc.vector.memset(w_planes[:].rearrange("p g n -> p (g n)").bitcast(I32), 0)
        nc.gpsimd.memset(logit_rows[N_TILES : 2 * N_TILES, :], 0.0)
        nc.gpsimd.memset(logit_rows[2 * N_TILES : P, :], 0.0)
        nc.vector.memset(a_rows[:], 0.0)
        nc.vector.memset(h_rows[:], 0.0)
        nc.vector.memset(warm[:], 0.0)
        nc.vector.memset(gate_pad[:].rearrange("p c j -> p (c j)").bitcast(I32), 0)

        nc.scalar.dma_start(out=t2_sb[:], in_=t2.partition_broadcast(P))
        nc.scalar.dma_start(out=logit_rows[0:N_TILES, :], in_=mlp_out.rearrange("(c p) e -> c (p e)", p=P))
        nc.scalar.dma_start(out=h_base_bf[:], in_=h[BASE].rearrange("(q t) -> q t", t=PACK))
        nc.scalar.activation(out=warm[:], in_=warm[:], func=ACT.Exp)

        for quad in range(4):
            nc.sync.dma_start(
                out=w_planes[32 * quad : 32 * quad + 4, :, :].bitcast(I32),
                in_=W_scales.bitcast(I32)[:, 4 * quad : 4 * quad + 4, :].rearrange("g r n -> r g n"),
            )
        z_raw = []

        def load_z(k):
            z_chunk = z_pool.tile([P, PACK, CHUNK], BF16)
            nc.sync.dma_start(out=z_chunk[:], in_=z_rows[:, :, k * CHUNK : (k + 1) * CHUNK])
            z_raw.append(z_chunk)

        load_z(0)
        for g in range(E):
            nc.sync.dma_start(
                out=w_words[:, g, :].bitcast(I32),
                in_=W_words[g].rearrange("p n t -> p (n t)").bitcast(I32),
            )
        nc.sync.dma_start(out=h_all[:], in_=h.partition_broadcast(P))
        for i in range(PIECES):
            nc.sync.dma_start(out=a_rows[E * i : E * (i + 1), :], in_=A)
            nc.sync.dma_start(out=h_rows[E * i : E * (i + 1), :], in_=h)
        for k in range(1, N_CHUNKS):
            load_z(k)

        ident_f = keep.tile([P, P], F32)
        make_identity(nc, ident_f[:])
        ident_b = keep.tile([P, P], BF16)
        make_identity(nc, ident_b[:])
        relu_flag = keep.tile([P, 1], F32)
        nc.vector.tensor_reduce(
            out=relu_flag[:], in_=ident_f[:, P - RELU_ROWS // PACK : P], axis=AX.X, op=ALU.add
        )
        floor = keep.tile([P, 1], F32)
        nc.vector.tensor_scalar(
            out=floor[:], in0=relu_flag[:], scalar1=BF16_MAX, scalar2=-BF16_MAX, op0=ALU.mult, op1=ALU.add
        )

        z_codes = keep.tile([P, B], U32, align_bytes=64)
        z_scales = keep.tile([P, B], U8, align_bytes=64)
        gate_rows = keep.tile([P, B], BF16)
        out_sb = {}
        grouped = {}
        leaves = {}
        mixed = {}
        scaled = {}
        h_tiles = {}
        back = {}
        h_pairs = {}
        mixed_a_ps = {}

        def tile_cols(c):
            return slice(c * P, (c + 1) * P)

        def cols_in_chunk(c):
            return slice((c % TILES_PER_CHUNK) * P, (c % TILES_PER_CHUNK + 1) * P)

        def regroup(c):
            first = (c % TILES_PER_CHUNK) * P
            grouped[c] = work.tile([P, 2 * P, PACK], BF16, align_bytes=64, name="grouped")
            nc.vector.tensor_scalar(
                out=grouped[c][:].rearrange("q (n i) t -> q n t i", i=RUN),
                in0=z_raw[c // TILES_PER_CHUNK][:, :, first : first + 2 * P].rearrange("q t (n i) -> q n t i", i=RUN),
                scalar1=floor[:, 0:1],
                scalar2=None,
                op0=ALU.max,
            )

        def quantise(c):
            nc.vector.quantize_mx(
                out=z_codes[:, c * P : (c + 2) * P].bitcast(FP8X4),
                scales=z_scales[:, c * P : (c + 2) * P],
                in_=grouped[c][:].rearrange("q b t -> q (b t)"),
            )

        def build_gate_rows(first):
            rows_ps = psum_g.tile([P, TILES_PER_BANK * P], BF16, tag="g_ps")
            for j in range(TILES_PER_BANK):
                nc.tensor.transpose(rows_ps[:, P * j : P * (j + 1)], gate_pad[:, first + j, :], ident_b[:])
            nc.scalar.copy(out=gate_rows[:, P * first : P * (first + TILES_PER_BANK)], in_=rows_ps[:])

        def chunk_cols(i):
            return slice((i // PACK) * CHUNK, (i // PACK + 1) * CHUNK)

        def mixed_a(i):
            mixed_a_ps[i] = psum_g.tile([P, CHUNK], F32, tag="g_ps", name="g_ps")
            nc.tensor.matmul(
                out=mixed_a_ps[i][:], lhsT=a_stat[:, i % PACK, :], rhs=gate_rows[:, chunk_cols(i)], start=True, stop=True
            )

        def a_term(i):
            if i % PACK == 0:
                out_sb[i // PACK] = out_pool.tile([P, PACK, CHUNK], F32, name="out_chunk")
            nc.vector.tensor_tensor(
                out=out_sb[i // PACK][:, i % PACK, :],
                in0=mixed_a_ps[i][:],
                in1=z_raw[i // PACK][:, i % PACK, :],
                op=ALU.mult,
            )

        def experts(c):
            leaves[c] = {}
            for e in (0, 2, 1, 3):
                p_ps = psum_p.tile([P, M], F32, name="p_ps%d" % e)
                nc.tensor.matmul_mx(
                    out=p_ps[:],
                    lhsT=z_codes[:, tile_cols(c)].bitcast(FP8X4),
                    lhsT_scale=z_scales[:, tile_cols(c)],
                    rhs=w_words[:, e, :].bitcast(FP8X4),
                    rhs_scale=w_planes[:, e, :],
                    start=True,
                    stop=True,
                )
                leaves[c][e] = p_ps[:].rearrange("b (q t) -> b t q", t=PACK)

        def mix_scalar(c):
            s0 = work.tile([P, PACK, P], F32)
            s2 = work.tile([P, PACK, P], F32)
            s3 = work.tile([P, SCALAR_GROUPS, P], F32)
            nc.scalar.activation(out=s0[:], in_=leaves[c][0], func=ACT.Copy, scale=gate[:, c, 0:1])
            nc.scalar.activation(out=s2[:], in_=leaves[c][2], func=ACT.Copy, scale=gate[:, c, 2:3])
            nc.scalar.activation(out=s3[:], in_=leaves[c][3][:, 0:SCALAR_GROUPS, :], func=ACT.Copy, scale=gate[:, c, 3:4])
            scaled[c] = (s0, s2, s3)

        def mix_first(c):
            s01 = work.tile([P, PACK, P], F32)
            nc.vector.scalar_tensor_tensor(
                out=s01[:], in0=leaves[c][1], scalar=gate[:, c, 1:2], in1=scaled[c][0][:], op0=ALU.mult, op1=ALU.add
            )
            s23_low = work.tile([P, SCALAR_GROUPS, P], F32)
            nc.gpsimd.tensor_tensor(
                out=s23_low[:], in0=scaled[c][1][:, 0:SCALAR_GROUPS, :], in1=scaled[c][2][:], op=ALU.add
            )
            mixed[c] = [s01, s23_low]

        def mix_second(c):
            s23_high = work.tile([P, PACK - SCALAR_GROUPS, P], F32)
            nc.vector.scalar_tensor_tensor(
                out=s23_high[:],
                in0=leaves[c][3][:, SCALAR_GROUPS:PACK, :],
                scalar=gate[:, c, 3:4],
                in1=scaled[c][1][:, SCALAR_GROUPS:PACK, :],
                op0=ALU.mult,
                op1=ALU.add,
            )
            all_high = work.tile([P, PACK - SCALAR_GROUPS, P], F32)
            nc.gpsimd.tensor_tensor(
                out=all_high[:], in0=mixed[c][0][:, SCALAR_GROUPS:PACK, :], in1=s23_high[:], op=ALU.add
            )
            mixed[c].append(all_high)

        def plain_groups(c):
            return PLAIN_H_GROUPS + (1 if c % EXTRA_PERIOD < EXTRA_TILES else 0)

        def gated_h(c):
            h_tiles[c] = []
            for e in range(BASE):
                gh = work.tile([P, PACK - plain_groups(c), P], F32, name="gh%d" % e)
                nc.scalar.activation(
                    out=gh[:],
                    in_=h_diff[:, e, plain_groups(c) - PLAIN_H_GROUPS :, :],
                    func=ACT.Copy,
                    scale=gate[:, c, e : e + 1],
                )
                h_tiles[c].append(gh)

        def pair_h(c):
            pair = work.tile([P, PACK - plain_groups(c), P], F32, name="pair")
            nc.gpsimd.tensor_tensor(out=pair[:], in0=h_tiles[c][0][:], in1=h_tiles[c][1][:], op=ALU.add)
            h_pairs[c] = [pair, h_tiles[c][2]]

        def turn_back(c):
            back[c] = psum_f.tile([P, PACK, P], F32, name="f_ps")
            s01, s23_low, all_high = mixed[c]
            for t in range(PACK):
                nc.tensor.matmul(
                    out=back[c][:, t, :],
                    lhsT=s01[:, t, :] if t < SCALAR_GROUPS else all_high[:, t - SCALAR_GROUPS, :],
                    rhs=ident_f[:],
                    start=(t == 0),
                    stop=False,
                    is_transpose=True,
                )
            for t in range(SCALAR_GROUPS):
                nc.tensor.matmul(
                    out=back[c][:, t, :], lhsT=s23_low[:, t, :], rhs=ident_f[:], start=False, stop=False, is_transpose=True
                )
            for part in h_pairs[c]:
                for t in range(plain_groups(c), PACK):
                    nc.tensor.matmul(
                        out=back[c][:, t, :],
                        lhsT=part[:, t - plain_groups(c), :],
                        rhs=ident_f[:],
                        start=False,
                        stop=False,
                        is_transpose=True,
                    )
            for t in range(plain_groups(c)):
                nc.tensor.matmul(
                    out=back[c][:, t, :],
                    lhsT=h_stat[:, t, :],
                    rhs=gate_rows[:, tile_cols(c)],
                    start=False,
                    stop=(t == plain_groups(c) - 1),
                )

        def finish(c):
            k = c // TILES_PER_CHUNK
            part = out_sb[k][:, 0 : plain_groups(c), cols_in_chunk(c)]
            nc.vector.tensor_tensor(out=part, in0=back[c][:, 0 : plain_groups(c), :], in1=part, op=ALU.add)
            for t in range(plain_groups(c), PACK):
                part = out_sb[k][:, t, cols_in_chunk(c)]
                nc.vector.scalar_tensor_tensor(
                    out=part, in0=back[c][:, t, :], scalar=h_base[:, t : t + 1], in1=part, op0=ALU.add, op1=ALU.add
                )
            if k == N_CHUNKS - 1:
                nc.sync.dma_start(out=out_rows[:, :, tile_cols(c)], in_=out_sb[k][:, :, cols_in_chunk(c)])
            elif c % TILES_PER_CHUNK == TILES_PER_CHUNK - 1:
                nc.sync.dma_start(out=out_rows[:, :, k * CHUNK : (k + 1) * CHUNK], in_=out_sb[k][:])

        t2_f = keep.tile([P, 1], F32)
        nc.vector.tensor_copy(out=t2_f[:], in_=t2_sb[:])
        inv_t2 = keep.tile([P, 1], F32)
        nc.vector.reciprocal(out=inv_t2[:], in_=t2_f[:])
        logit_ps = psum_g.tile([P, E, P], BF16, tag="g_ps")
        for e in range(E):
            nc.tensor.transpose(logit_ps[:, e, :], logit_rows[:].rearrange("c (p e) -> c e p", e=E)[:, e, :], ident_b[:])
        logit = keep.tile([P, N_TILES, E], F32)
        nc.vector.tensor_scalar(
            out=logit[:],
            in0=logit_ps[:, :, 0:N_TILES].rearrange("p e c -> p c e"),
            scalar1=inv_t2[:, 0:1],
            scalar2=-1.0,
            op0=ALU.mult,
            op1=ALU.mult,
        )
        top = keep.tile([P, N_TILES], F32)
        nc.vector.tensor_reduce(out=top[:], in_=logit[:], axis=AX.X, op=ALU.max)
        nc.vector.tensor_tensor(
            out=logit[:], in0=logit[:], in1=top[:].unsqueeze(2).to_broadcast([P, N_TILES, E]), op=ALU.subtract
        )
        expd = keep.tile([P, N_TILES, E], F32)
        nc.scalar.activation(out=expd[:], in_=logit[:], func=ACT.Exp)
        regroup(0)
        total = keep.tile([P, N_TILES], F32)
        nc.vector.tensor_reduce(out=total[:], in_=expd[:], axis=AX.X, op=ALU.add)
        quantise(0)
        experts(0)
        inv_total = keep.tile([P, N_TILES], F32)
        nc.vector.reciprocal(out=inv_total[:], in_=total[:])
        gate = keep.tile([P, N_TILES, E], F32)
        nc.vector.tensor_tensor(
            out=gate[:], in0=expd[:], in1=inv_total[:].unsqueeze(2).to_broadcast([P, N_TILES, E]), op=ALU.mult
        )

        regroup(2)

        rest = gate
        for i in range(PIECES):
            piece = gate_pad[:, :, E * i : E * (i + 1)]
            nc.vector.tensor_copy(out=piece, in_=rest[:])
            if i + 1 < PIECES:
                smaller = keep.tile([P, N_TILES, E], F32, name="rest%d" % i)
                nc.vector.tensor_tensor(out=smaller[:], in0=rest[:], in1=piece, op=ALU.subtract)
                rest = smaller
        a_stat = keep.tile([P, PACK, P], BF16)
        h_stat = keep.tile([P, PACK, P], BF16)
        nc.vector.tensor_copy(out=a_stat[:], in_=a_rows[:].rearrange("j (q t) -> j t q", t=PACK))
        nc.vector.tensor_copy(out=h_stat[:], in_=h_rows[:].rearrange("j (q t) -> j t q", t=PACK))

        def engine_groups(e):
            return h_all[:, e, :].rearrange("b (q t) -> b t q", t=PACK)[:, PLAIN_H_GROUPS:PACK, :]

        h_diff = keep.tile([P, BASE, PACK - PLAIN_H_GROUPS, P], F32)
        for e in range(BASE):
            nc.vector.tensor_tensor(out=h_diff[:, e, :, :], in0=engine_groups(e), in1=engine_groups(BASE), op=ALU.subtract)
        h_base = keep.tile([P, PACK], F32)
        nc.vector.tensor_copy(out=h_base[:], in_=h_base_bf[:])

        for c in range(N_TILES + 3):
            if 1 <= c < N_TILES + 1:
                pair_h(c - 1)
            if c < N_TILES:
                mix_scalar(c)
                mix_first(c)
                gated_h(c)
            if c >= 3:
                finish(c - 3)
            if c < N_TILES:
                mix_second(c)
            if (c + 2) % TILES_PER_BANK == ROWS_AHEAD and c + 2 + ROWS_AHEAD < N_TILES:
                build_gate_rows(c + 2 + ROWS_AHEAD)
            if 2 <= c < N_TILES + 2:
                turn_back(c - 2)
            if c == 0:
                build_gate_rows(0)
                mixed_a(0)
                a_term(0)
                mixed_a(1)
            if c + 1 < N_TILES:
                a_term(c + 1)
                experts(c + 1)
            if c + 2 < N_TILES:
                mixed_a(c + 2)
            if c % 2 == 0 and c + 2 < N_TILES:
                quantise(c + 2)
            if c % 2 == 1 and c + 3 < N_TILES:
                regroup(c + 3)
